import numpy as np
import ml_dtypes


def mxq(x, axis, fmt="e4m3"):
    dtype, down = {"e4m3": (ml_dtypes.float8_e4m3fn, 7), "e5m2": (ml_dtypes.float8_e5m2, 14)}[fmt]
    v = np.moveaxis(np.asarray(x, np.float32).astype(ml_dtypes.bfloat16).astype(np.float64), axis, -1)
    blocks = v.reshape(v.shape[:-1] + (-1, 32))
    amax = np.abs(blocks).max(-1, keepdims=True)
    byte = np.maximum(np.where(amax > 0, np.frexp(amax)[1] - 1 + 127, 0) - down, 1)
    scale = np.exp2(byte - 127.0)
    codes = (blocks / scale).astype(np.float32).astype(dtype).astype(np.float64)
    return np.moveaxis((codes * scale).reshape(v.shape), -1, axis)


WIDE = False


def mx_kscale(k):
    if not WIDE:
        return np.ones(k)
    levels = np.array([10, -10, 5, -5, 0])
    a = np.random.permutation(np.resize(levels, k // 512 * 4)).reshape(k // 512, 4)
    idx = np.arange(k)
    return np.exp2(a[idx // 512, idx % 128 // 32])


BF16 = ml_dtypes.bfloat16


def bf(x):
    return np.asarray(x, np.float32).astype(BF16)


def f64(x):
    return np.asarray(x).astype(np.float64)


E2M1 = np.array([0.0, 0.5, 1.0, 1.5, 2.0, 3.0, 4.0, 6.0, -0.0, -0.5, -1.0, -1.5, -2.0, -3.0, -4.0, -6.0])


def pack_weight(w, fmt):
    k, n = w.shape
    w = f64(bf(w)).reshape(k // 32, 32, n)
    amax = np.abs(w).max(1)
    if fmt == "e4m3":
        byte = np.frexp(amax)[1] - 1 + 127 - 7
    else:
        mant, ex = np.frexp(amax / 6.0)
        byte = np.where(mant > 0.5, ex, ex - 1) + 127
    byte = np.clip(np.where(amax > 0, byte, 1), 1, 254)
    scaled = (w * np.exp2(127.0 - byte)[:, None, :]).reshape(k, n).astype(np.float32)
    by_word = np.ascontiguousarray(scaled.reshape(k // 512, 128, 4, n).transpose(0, 1, 3, 2))
    if fmt == "e4m3":
        words = by_word.astype(ml_dtypes.float8_e4m3fn).view(np.uint8)
    else:
        c = by_word.astype(ml_dtypes.float4_e2m1fn).view(np.uint8) & 0xF
        words = c[..., 0::2] | (c[..., 1::2] << 4)
    return np.ascontiguousarray(words), np.ascontiguousarray(byte.astype(np.uint8).reshape(k // 512, 16, n))


def unpack_weight(words, scales, fmt):
    g, p, n, _ = words.shape
    if fmt == "e4m3":
        vals = np.ascontiguousarray(words).view(ml_dtypes.float8_e4m3fn).astype(np.float64)
    else:
        nib = np.empty((g, p, n, 4), np.uint8)
        nib[..., 0::2] = words & 0xF
        nib[..., 1::2] = words >> 4
        vals = E2M1[nib]
    vals = vals * np.repeat(np.exp2(scales.astype(np.float64) - 127.0), 8, axis=1)[..., None]
    return vals.transpose(0, 1, 3, 2).reshape(g * 512, n)


B, E, LATENT, COND, HIDDEN, OUT, GH = 1024, 8, 128, 384, 384, 256, 128
INPUT = LATENT + COND
EPS = 1e-5


def elu(v):
    return np.where(v > 0.0, v, np.exp(np.minimum(v, 0.0)) - 1.0)


def layernorm(v):
    mu = v.mean(-1, keepdims=True)
    var = np.square(v - mu).mean(-1, keepdims=True)
    return (v - mu) / np.sqrt(var + EPS)


def softmax(v):
    e = np.exp(v - v.max(-1, keepdims=True))
    return e / e.sum(-1, keepdims=True)


def setup_inputs():
    rn = np.random.standard_normal
    swap = np.arange(INPUT) ^ 1
    s = f64(mx_kscale(INPUT))
    s = np.minimum(s, s[swap])
    g = np.exp2(np.round(np.log2(np.sqrt(np.mean(s * s)))))
    u = rn((B, INPUT))
    pair = f64(bf((u - u[:, swap]) * np.sqrt(0.5)))
    gen = np.concatenate([0.5 * rn((B, LATENT)), 0.4 + rn((B, COND))], axis=1)
    x = pair * s + np.min(s) ** 3 * gen
    gate_logits = bf(1.5 * rn((B, E)))
    w0 = rn((E, INPUT, HIDDEN)) * 1.5 / np.sqrt(INPUT) / s[None, :, None] * g
    w0_words, w0_scales = pack_weight(w0.reshape(-1, HIDDEN), "e4m3")
    b0 = bf(rn((E, HIDDEN)) * 0.5)
    return {"z": bf(x[:, :LATENT]),
            "c": bf(x[:, LATENT:]),
            "gate_logits": gate_logits,
            "w0_words": w0_words,
            "w0_scales": w0_scales,
            "b0": b0}


def reference(z, c, gate_logits, w0_words, w0_scales, b0):
    coeff = softmax(f64(gate_logits))
    inp = layernorm(np.concatenate([f64(z), f64(c)], axis=-1))
    y = mxq(inp, 1, "e4m3") @ unpack_weight(w0_words, w0_scales, "e4m3").reshape(E, INPUT, HIDDEN)
    mixed = (coeff.T[:, :, None] * y).sum(0)
    mixed_bias = (coeff[:, :, None] * f64(b0)[None]).sum(1)
    return elu(mixed + mixed_bias)

@@ -1,0 +1,187 @@
+import concourse.mybir as mybir
+from concourse.masks import make_identity
+
+F32 = mybir.dt.float32
+BF16 = mybir.dt.bfloat16
+I32 = mybir.dt.int32
+U32 = mybir.dt.uint32
+U8 = mybir.dt.uint8
+FP8X4 = mybir.dt.float8_e4m3fn_x4
+ALU = mybir.AluOpType
+ACT = mybir.ActivationFunctionType
+AXIS = mybir.AxisListType
+
+P = 128
+ROWS = 1024
+EXPERTS = 8
+LATENT = 128
+FEATURES = 512
+PACK = 4
+HIDDEN = 384
+EPS = 1e-5
+TILES = ROWS // P
+PAIR = 2
+HALF = TILES // 2
+N_WIDE = 256
+SPLIT = 2
+
+FLOPS = 2 * ROWS * FEATURES * HIDDEN * EXPERTS + 2 * ROWS * EXPERTS * HIDDEN
+
+
+def tile_gatingmixeddecoder_pa_e_kernel(tc, z, c, gate_logits, w0_words, w0_scales, b0, out):
+    nc = tc.nc
+    z_rows = z.rearrange("(p t) k -> p t k", t=TILES)
+    c_rows = c.rearrange("(p t) k -> p t k", t=TILES)
+    gate_rows = gate_logits.rearrange("(p t) e -> p t e", t=TILES)
+    out_rows = out.rearrange("(p t) n -> p t n", t=TILES)
+    words_dram = w0_words.rearrange("g p n t -> g p (n t)").bitcast(I32).rearrange("g p n -> p g n")
+    scales_dram = w0_scales.bitcast(I32).rearrange("g q n -> q g n")
+
+    with tc.tile_pool(name="keep", bufs=1) as keep, tc.tile_pool(name="work", bufs=2) as work, tc.psum_pool(
+        name="flip", bufs=2
+    ) as flip, tc.psum_pool(name="prod", bufs=6) as prod:
+        x_sb = keep.tile([P, TILES, FEATURES], BF16)
+        gate_sb = keep.tile([P, TILES, EXPERTS], BF16)
+        w_words = keep.tile([P, EXPERTS, HIDDEN], U32, align_bytes=64)
+        w_planes = keep.tile([P, EXPERTS, HIDDEN], U8, align_bytes=64)
+        b_rep = keep.tile([P, HIDDEN], BF16)
+        ident = keep.tile([P, P], BF16)
+        neg_half = keep.tile([P, PAIR], F32)
+
+        nc.vector.memset(w_planes[:].bitcast(I32), 0)
+        nc.vector.memset(neg_half[:], -0.5)
+
+        nc.gpsimd.dma_start(out=gate_sb[:], in_=gate_rows)
+        make_identity(nc, ident[:])
+        nc.gpsimd.dma_start(out=b_rep[:], in_=b0.unsqueeze(0).to_broadcast([P // EXPERTS, EXPERTS, HIDDEN]))
+        for h in range(TILES // HALF):
+            ts = slice(h * HALF, (h + 1) * HALF)
+            nc.sync.dma_start(out=x_sb[:, ts, 0:LATENT], in_=z_rows[:, ts, :])
+            nc.sync.dma_start(out=x_sb[:, ts, LATENT:FEATURES], in_=c_rows[:, ts, :])
+        for quad in range(4):
+            nc.sync.dma_start(
+                out=w_planes[32 * quad : 32 * quad + 4].bitcast(I32), in_=scales_dram[4 * quad : 4 * quad + 4]
+            )
+        for e in range(0, EXPERTS, 2):
+            nc.sync.dma_start(out=w_words[:, e : e + 2, :].bitcast(I32), in_=words_dram[:, e : e + 2, :])
+
+        gate_max = keep.tile([P, TILES], F32)
+        nc.vector.tensor_reduce(out=gate_max[:], in_=gate_sb[:], axis=AXIS.X, op=ALU.max)
+        shifted = keep.tile([P, TILES, EXPERTS], F32)
+        nc.vector.tensor_tensor(
+            out=shifted[:],
+            in0=gate_sb[:],
+            in1=gate_max[:].unsqueeze(2).to_broadcast([P, TILES, EXPERTS]),
+            op=ALU.subtract,
+        )
+        expd = keep.tile([P, TILES, EXPERTS], F32)
+        nc.scalar.activation(out=expd[:], in_=shifted[:], func=ACT.Exp)
+        exp_sum = keep.tile([P, TILES], F32)
+        nc.vector.tensor_reduce(out=exp_sum[:], in_=expd[:], axis=AXIS.X, op=ALU.add)
+        inv_sum = keep.tile([P, TILES], F32)
+        nc.vector.reciprocal(out=inv_sum[:], in_=exp_sum[:])
+        coeff = keep.tile([P, TILES, EXPERTS], F32)
+        nc.vector.tensor_tensor(
+            out=coeff[:],
+            in0=expd[:],
+            in1=inv_sum[:].unsqueeze(2).to_broadcast([P, TILES, EXPERTS]),
+            op=ALU.mult,
+        )
+
+        c_split = keep.tile([P, TILES, SPLIT, EXPERTS], BF16)
+        nc.vector.tensor_copy(out=c_split[:, :, 0, :], in_=coeff[:])
+        nc.vector.tensor_tensor(out=c_split[:, :, 1, :], in0=coeff[:], in1=c_split[:, :, 0, :], op=ALU.subtract)
+        c_flip = flip.tile([P, P], BF16, tag="flip")
+        nc.tensor.transpose(c_flip[:], c_split[:].rearrange("p t h e -> p (t h e)"), ident[:])
+        own_tile = keep.tile([P, TILES], F32)
+        nc.vector.tensor_reduce(
+            out=own_tile[:], in_=ident[:].rearrange("q (t j) -> q t j", t=TILES), axis=AXIS.X, op=ALU.add
+        )
+        c_lhsT = keep.tile([P, TILES, P], BF16)
+        nc.vector.tensor_tensor(
+            out=c_lhsT[:],
+            in0=c_flip[:].unsqueeze(1).to_broadcast([P, TILES, P]),
+            in1=own_tile[:].unsqueeze(2).to_broadcast([P, TILES, P]),
+            op=ALU.mult,
+        )
+        bias_sb = keep.tile([P, TILES, HIDDEN], F32)
+        for t in range(TILES):
+            bias_ps = prod.tile([P, HIDDEN], F32, tag="prod")
+            nc.tensor.matmul(out=bias_ps[:], lhsT=c_lhsT[:, t, :], rhs=b_rep[:], start=True, stop=True)
+            nc.scalar.copy(out=bias_sb[:, t, :], in_=bias_ps[:])
+
+        stats = keep.tile([P, TILES, 6], F32)
+        mean_var = keep.tile([P, TILES, 2], F32)
+        var_eps = keep.tile([P, TILES], F32)
+        rstd = keep.tile([P, TILES], F32)
+        inp = keep.tile([P, TILES, FEATURES], BF16)
+        a_words = keep.tile([P, TILES, P], U32, align_bytes=64)
+        a_planes = keep.tile([P, TILES, P], U8, align_bytes=64)
+        for t0 in range(0, TILES, PAIR):
+            pair = slice(t0, t0 + PAIR)
+            for t in range(t0, t0 + PAIR):
+                nc.vector.bn_stats(out=stats[:, t, :], in_=x_sb[:, t, :])
+                nc.vector.bn_aggr(out=mean_var[:, t, :], in_=stats[:, t, :])
+            nc.gpsimd.tensor_scalar(
+                out=var_eps[:, pair], in0=mean_var[:, pair, 1], scalar1=EPS, scalar2=1.0, op0=ALU.add, op1=ALU.mult
+            )
+            nc.gpsimd.tensor_tensor(out=rstd[:, pair], in0=var_eps[:, pair], in1=neg_half[:], op=ALU.pow)
+            for t in range(t0, t0 + PAIR):
+                nc.vector.tensor_scalar(
+                    out=inp[:, t, :],
+                    in0=x_sb[:, t, :],
+                    scalar1=mean_var[:, t, 0:1],
+                    scalar2=rstd[:, t : t + 1],
+                    op0=ALU.subtract,
+                    op1=ALU.mult,
+                )
+            flipped = flip.tile([P, PAIR, PACK, P], BF16, tag="flip")
+            for a in range(PAIR):
+                for j in range(PACK):
+                    nc.tensor.transpose(flipped[:, a, j, :], inp[:, t0 + a, j:FEATURES:PACK], ident[:])
+            grouped = work.tile([P, PAIR, P, PACK], BF16, align_bytes=64)
+            nc.scalar.copy(out=grouped[:], in_=flipped[:].rearrange("p a j r -> p a r j"))
+            nc.vector.quantize_mx(
+                out=a_words[:, pair, :].rearrange("p a r -> p (a r)").bitcast(FP8X4),
+                scales=a_planes[:, pair, :].rearrange("p a r -> p (a r)"),
+                in_=grouped[:].rearrange("p a r j -> p (a r j)"),
+            )
+
+        mixed = keep.tile([P, TILES, HIDDEN], F32)
+        result = keep.tile([P, TILES, HIDDEN], F32)
+        for t0 in range(0, TILES, PAIR):
+            pair = slice(t0, t0 + PAIR)
+            for e in range(EXPERTS):
+                for t in range(t0, t0 + PAIR):
+                    y = prod.tile([P, HIDDEN], F32, tag="prod")
+                    for cols in (slice(0, N_WIDE), slice(N_WIDE, HIDDEN)):
+                        nc.tensor.matmul_mx(
+                            out=y[:, cols],
+                            lhsT=a_words[:, t, :].bitcast(FP8X4),
+                            lhsT_scale=a_planes[:, t, :],
+                            rhs=w_words[:, e, cols].bitcast(FP8X4),
+                            rhs_scale=w_planes[:, e, cols],
+                            start=True,
+                            stop=True,
+                        )
+                    nc.vector.scalar_tensor_tensor(
+                        out=mixed[:, t, :],
+                        in0=y[:],
+                        scalar=coeff[:, t, e : e + 1],
+                        in1=bias_sb[:, t, :] if e == 0 else mixed[:, t, :],
+                        op0=ALU.mult,
+                        op1=ALU.add,
+                    )
+            below = work.tile([P, PAIR, HIDDEN], F32)
+            nc.scalar.activation(out=below[:], in_=mixed[:, pair, :], func=ACT.Relu, scale=-1.0)
+            grown = work.tile([P, PAIR, HIDDEN], F32)
+            nc.scalar.activation(out=grown[:], in_=below[:], func=ACT.Exp, scale=-1.0)
+            nc.vector.scalar_tensor_tensor(
+                out=result[:, pair, :],
+                in0=grown[:],
+                scalar=-1.0,
+                in1=mixed[:, pair, :],
+                op0=ALU.add,
+                op1=ALU.max,
+            )
+            nc.sync.dma_start(out=out_rows[:, pair, :], in_=result[:, pair, :])

@@ -21,9 +21,12 @@ HIDDEN = 384
 EPS = 1e-5
 TILES = ROWS // P
 PAIR = 2
+PAIRS = TILES // PAIR
 HALF = TILES // 2
 N_WIDE = 256
 SPLIT = 2
+SIDE_EXPERTS = 2
+OWN_EXPERTS = EXPERTS - SIDE_EXPERTS
 
 FLOPS = 2 * ROWS * FEATURES * HIDDEN * EXPERTS + 2 * ROWS * EXPERTS * HIDDEN
 
@@ -37,9 +40,9 @@ def tile_gatingmixeddecoder_pa_e_kernel(tc, z, c, gate_logits, w0_words, w0_scal
     words_dram = w0_words.rearrange("g p n t -> g p (n t)").bitcast(I32).rearrange("g p n -> p g n")
     scales_dram = w0_scales.bitcast(I32).rearrange("g q n -> q g n")
 
-    with tc.tile_pool(name="keep", bufs=1) as keep, tc.tile_pool(name="work", bufs=2) as work, tc.psum_pool(
+    with tc.tile_pool(name="keep", bufs=1) as keep, tc.tile_pool(name="work", bufs=4) as work, tc.psum_pool(
         name="flip", bufs=2
-    ) as flip, tc.psum_pool(name="prod", bufs=6) as prod:
+    ) as flip, tc.psum_pool(name="lent", bufs=2) as lent, tc.psum_pool(name="own", bufs=4) as own:
         x_sb = keep.tile([P, TILES, FEATURES], BF16)
         gate_sb = keep.tile([P, TILES, EXPERTS], BF16)
         w_words = keep.tile([P, EXPERTS, HIDDEN], U32, align_bytes=64)
@@ -51,9 +54,7 @@ def tile_gatingmixeddecoder_pa_e_kernel(tc, z, c, gate_logits, w0_words, w0_scal
         nc.vector.memset(w_planes[:].bitcast(I32), 0)
         nc.vector.memset(neg_half[:], -0.5)
 
-        nc.gpsimd.dma_start(out=gate_sb[:], in_=gate_rows)
-        make_identity(nc, ident[:])
-        nc.gpsimd.dma_start(out=b_rep[:], in_=b0.unsqueeze(0).to_broadcast([P // EXPERTS, EXPERTS, HIDDEN]))
+        nc.sync.dma_start(out=gate_sb[:], in_=gate_rows)
         for h in range(TILES // HALF):
             ts = slice(h * HALF, (h + 1) * HALF)
             nc.sync.dma_start(out=x_sb[:, ts, 0:LATENT], in_=z_rows[:, ts, :])
@@ -64,6 +65,14 @@ def tile_gatingmixeddecoder_pa_e_kernel(tc, z, c, gate_logits, w0_words, w0_scal
             )
         for e in range(0, EXPERTS, 2):
             nc.sync.dma_start(out=w_words[:, e : e + 2, :].bitcast(I32), in_=words_dram[:, e : e + 2, :])
+        make_identity(nc, ident[:])
+        nc.gpsimd.dma_start(out=b_rep[:], in_=b0.unsqueeze(0).to_broadcast([P // EXPERTS, EXPERTS, HIDDEN]))
+
+        def tiles_of(i):
+            return range(i * PAIR, (i + 1) * PAIR)
+
+        def pair_of(i):
+            return slice(i * PAIR, (i + 1) * PAIR)
 
         gate_max = keep.tile([P, TILES], F32)
         nc.vector.tensor_reduce(out=gate_max[:], in_=gate_sb[:], axis=AXIS.X, op=ALU.max)
@@ -91,42 +100,43 @@ def tile_gatingmixeddecoder_pa_e_kernel(tc, z, c, gate_logits, w0_words, w0_scal
         c_split = keep.tile([P, TILES, SPLIT, EXPERTS], BF16)
         nc.vector.tensor_copy(out=c_split[:, :, 0, :], in_=coeff[:])
         nc.vector.tensor_tensor(out=c_split[:, :, 1, :], in0=coeff[:], in1=c_split[:, :, 0, :], op=ALU.subtract)
-        c_flip = flip.tile([P, P], BF16, tag="flip")
-        nc.tensor.transpose(c_flip[:], c_split[:].rearrange("p t h e -> p (t h e)"), ident[:])
         own_tile = keep.tile([P, TILES], F32)
         nc.vector.tensor_reduce(
             out=own_tile[:], in_=ident[:].rearrange("q (t j) -> q t j", t=TILES), axis=AXIS.X, op=ALU.add
         )
+        c_flip = flip.tile([P, P], BF16, tag="flip")
+        nc.tensor.transpose(c_flip[:], c_split[:].rearrange("p t h e -> p (t h e)"), ident[:])
         c_lhsT = keep.tile([P, TILES, P], BF16)
-        nc.vector.tensor_tensor(
-            out=c_lhsT[:],
-            in0=c_flip[:].unsqueeze(1).to_broadcast([P, TILES, P]),
-            in1=own_tile[:].unsqueeze(2).to_broadcast([P, TILES, P]),
-            op=ALU.mult,
-        )
-        bias_sb = keep.tile([P, TILES, HIDDEN], F32)
         for t in range(TILES):
-            bias_ps = prod.tile([P, HIDDEN], F32, tag="prod")
+            nc.scalar.activation(out=c_lhsT[:, t, :], in_=c_flip[:], func=ACT.Copy, scale=own_tile[:, t : t + 1])
+        side = keep.tile([P, TILES, HIDDEN], F32)
+        for t in range(TILES):
+            bias_ps = lent.tile([P, HIDDEN], F32, tag="lent")
             nc.tensor.matmul(out=bias_ps[:], lhsT=c_lhsT[:, t, :], rhs=b_rep[:], start=True, stop=True)
-            nc.scalar.copy(out=bias_sb[:, t, :], in_=bias_ps[:])
+            nc.scalar.copy(out=side[:, t, :], in_=bias_ps[:])
 
         stats = keep.tile([P, TILES, 6], F32)
         mean_var = keep.tile([P, TILES, 2], F32)
         var_eps = keep.tile([P, TILES], F32)
         rstd = keep.tile([P, TILES], F32)
         inp = keep.tile([P, TILES, FEATURES], BF16)
+        grouped = keep.tile([P, TILES, P, PACK], BF16, align_bytes=64)
         a_words = keep.tile([P, TILES, P], U32, align_bytes=64)
         a_planes = keep.tile([P, TILES, P], U8, align_bytes=64)
-        for t0 in range(0, TILES, PAIR):
-            pair = slice(t0, t0 + PAIR)
-            for t in range(t0, t0 + PAIR):
+        for i in range(PAIRS):
+            for t in tiles_of(i):
                 nc.vector.bn_stats(out=stats[:, t, :], in_=x_sb[:, t, :])
                 nc.vector.bn_aggr(out=mean_var[:, t, :], in_=stats[:, t, :])
             nc.gpsimd.tensor_scalar(
-                out=var_eps[:, pair], in0=mean_var[:, pair, 1], scalar1=EPS, scalar2=1.0, op0=ALU.add, op1=ALU.mult
+                out=var_eps[:, pair_of(i)],
+                in0=mean_var[:, pair_of(i), 1],
+                scalar1=EPS,
+                scalar2=1.0,
+                op0=ALU.add,
+                op1=ALU.mult,
             )
-            nc.gpsimd.tensor_tensor(out=rstd[:, pair], in0=var_eps[:, pair], in1=neg_half[:], op=ALU.pow)
-            for t in range(t0, t0 + PAIR):
+            nc.gpsimd.tensor_tensor(out=rstd[:, pair_of(i)], in0=var_eps[:, pair_of(i)], in1=neg_half[:], op=ALU.pow)
+            for t in tiles_of(i):
                 nc.vector.tensor_scalar(
                     out=inp[:, t, :],
                     in0=x_sb[:, t, :],
@@ -136,52 +146,67 @@ def tile_gatingmixeddecoder_pa_e_kernel(tc, z, c, gate_logits, w0_words, w0_scal
                     op1=ALU.mult,
                 )
             flipped = flip.tile([P, PAIR, PACK, P], BF16, tag="flip")
-            for a in range(PAIR):
+            for a, t in enumerate(tiles_of(i)):
                 for j in range(PACK):
-                    nc.tensor.transpose(flipped[:, a, j, :], inp[:, t0 + a, j:FEATURES:PACK], ident[:])
-            grouped = work.tile([P, PAIR, P, PACK], BF16, align_bytes=64)
-            nc.scalar.copy(out=grouped[:], in_=flipped[:].rearrange("p a j r -> p a r j"))
+                    nc.tensor.transpose(flipped[:, a, j, :], inp[:, t, j:FEATURES:PACK], ident[:])
+            nc.scalar.copy(out=grouped[:, pair_of(i)], in_=flipped[:].rearrange("p a j r -> p a r j"))
             nc.vector.quantize_mx(
-                out=a_words[:, pair, :].rearrange("p a r -> p (a r)").bitcast(FP8X4),
-                scales=a_planes[:, pair, :].rearrange("p a r -> p (a r)"),
-                in_=grouped[:].rearrange("p a r j -> p (a r j)"),
+                out=a_words[:, pair_of(i), :].rearrange("p a r -> p (a r)").bitcast(FP8X4),
+                scales=a_planes[:, pair_of(i), :].rearrange("p a r -> p (a r)"),
+                in_=grouped[:, pair_of(i)].rearrange("p a r j -> p (a r j)"),
             )
 
         mixed = keep.tile([P, TILES, HIDDEN], F32)
         result = keep.tile([P, TILES, HIDDEN], F32)
-        for t0 in range(0, TILES, PAIR):
-            pair = slice(t0, t0 + PAIR)
-            for e in range(EXPERTS):
-                for t in range(t0, t0 + PAIR):
-                    y = prod.tile([P, HIDDEN], F32, tag="prod")
-                    for cols in (slice(0, N_WIDE), slice(N_WIDE, HIDDEN)):
-                        nc.tensor.matmul_mx(
-                            out=y[:, cols],
-                            lhsT=a_words[:, t, :].bitcast(FP8X4),
-                            lhsT_scale=a_planes[:, t, :],
-                            rhs=w_words[:, e, cols].bitcast(FP8X4),
-                            rhs_scale=w_planes[:, e, cols],
-                            start=True,
-                            stop=True,
-                        )
+
+        def product(y, t, e):
+            for cols in (slice(0, N_WIDE), slice(N_WIDE, HIDDEN)):
+                nc.tensor.matmul_mx(
+                    out=y[:, cols],
+                    lhsT=a_words[:, t, :].bitcast(FP8X4),
+                    lhsT_scale=a_planes[:, t, :],
+                    rhs=w_words[:, e, cols].bitcast(FP8X4),
+                    rhs_scale=w_planes[:, e, cols],
+                    start=True,
+                    stop=True,
+                )
+
+        def side_terms(i):
+            for e in range(OWN_EXPERTS, EXPERTS):
+                for t in tiles_of(i):
+                    y_lent = lent.tile([P, HIDDEN], F32, tag="lent")
+                    product(y_lent, t, e)
+                    part = work.tile([P, HIDDEN], F32)
+                    nc.scalar.activation(out=part[:], in_=y_lent[:], func=ACT.Copy, scale=coeff[:, t, e : e + 1])
+                    nc.gpsimd.tensor_tensor(out=side[:, t, :], in0=side[:, t, :], in1=part[:], op=ALU.add)
+
+        def own_terms(i, experts):
+            for e in range(experts):
+                for t in tiles_of(i):
+                    y_own = own.tile([P, HIDDEN], F32, tag="own")
+                    product(y_own, t, e)
                     nc.vector.scalar_tensor_tensor(
                         out=mixed[:, t, :],
-                        in0=y[:],
+                        in0=y_own[:],
                         scalar=coeff[:, t, e : e + 1],
-                        in1=bias_sb[:, t, :] if e == 0 else mixed[:, t, :],
+                        in1=side[:, t, :] if e == 0 else mixed[:, t, :],
                         op0=ALU.mult,
                         op1=ALU.add,
                     )
-            below = work.tile([P, PAIR, HIDDEN], F32)
-            nc.scalar.activation(out=below[:], in_=mixed[:, pair, :], func=ACT.Relu, scale=-1.0)
-            grown = work.tile([P, PAIR, HIDDEN], F32)
-            nc.scalar.activation(out=grown[:], in_=below[:], func=ACT.Exp, scale=-1.0)
-            nc.vector.scalar_tensor_tensor(
-                out=result[:, pair, :],
-                in0=grown[:],
-                scalar=-1.0,
-                in1=mixed[:, pair, :],
-                op0=ALU.add,
-                op1=ALU.max,
-            )
-            nc.sync.dma_start(out=out_rows[:, pair, :], in_=result[:, pair, :])
+
+        def elu(i):
+            for t in tiles_of(i):
+                below = work.tile([P, HIDDEN], F32)
+                nc.scalar.activation(out=below[:], in_=mixed[:, t, :], func=ACT.Relu, scale=-1.0)
+                grown = work.tile([P, HIDDEN], F32)
+                nc.scalar.activation(out=grown[:], in_=below[:], func=ACT.Exp, scale=-1.0)
+                nc.vector.scalar_tensor_tensor(
+                    out=result[:, t, :], in0=grown[:], scalar=-1.0, in1=mixed[:, t, :], op0=ALU.add, op1=ALU.max
+                )
+                nc.sync.dma_start(out=out_rows[:, t, :], in_=result[:, t, :])
+
+        for i in range(PAIRS):
+            if i + 1 < PAIRS:
+                side_terms(i + 1)
+            own_terms(i, EXPERTS if i == 0 else OWN_EXPERTS)
+            elu(i)

@@ -194,19 +194,28 @@ def tile_gatingmixeddecoder_pa_e_kernel(tc, z, c, gate_logits, w0_words, w0_scal
                         op1=ALU.add,
                     )
 
-        def elu(i):
+        grown = keep.tile([P, TILES, HIDDEN], F32)
+
+        def elu_head(i):
             for t in tiles_of(i):
                 below = work.tile([P, HIDDEN], F32)
                 nc.scalar.activation(out=below[:], in_=mixed[:, t, :], func=ACT.Relu, scale=-1.0)
-                grown = work.tile([P, HIDDEN], F32)
-                nc.scalar.activation(out=grown[:], in_=below[:], func=ACT.Exp, scale=-1.0)
+                nc.scalar.activation(out=grown[:, t, :], in_=below[:], func=ACT.Exp, scale=-1.0)
+
+        def elu_tail(i):
+            for t in tiles_of(i):
                 nc.vector.scalar_tensor_tensor(
-                    out=result[:, t, :], in0=grown[:], scalar=-1.0, in1=mixed[:, t, :], op0=ALU.add, op1=ALU.max
+                    out=result[:, t, :], in0=grown[:, t, :], scalar=-1.0, in1=mixed[:, t, :], op0=ALU.add, op1=ALU.max
                 )
                 nc.sync.dma_start(out=out_rows[:, t, :], in_=result[:, t, :])
 
+        LAST = PAIRS - 1
         for i in range(PAIRS):
-            if i + 1 < PAIRS:
+            if i < LAST:
                 side_terms(i + 1)
             own_terms(i, EXPERTS if i == 0 else OWN_EXPERTS)
-            elu(i)
+            elu_head(i)
+            if i + 1 == LAST:
+                for earlier in range(LAST):
+                    elu_tail(earlier)
+        elu_tail(LAST)

@@ -126,6 +126,7 @@ def tile_gatingmixeddecoder_pa_e_kernel(tc, z, c, gate_logits, w0_words, w0_scal
         for i in range(PAIRS):
             for t in tiles_of(i):
                 nc.vector.bn_stats(out=stats[:, t, :], in_=x_sb[:, t, :])
+            for t in tiles_of(i):
                 nc.vector.bn_aggr(out=mean_var[:, t, :], in_=stats[:, t, :])
             nc.gpsimd.tensor_scalar(
                 out=var_eps[:, pair_of(i)],
@@ -216,6 +217,6 @@ def tile_gatingmixeddecoder_pa_e_kernel(tc, z, c, gate_logits, w0_words, w0_scal
             own_terms(i, EXPERTS if i == 0 else OWN_EXPERTS)
             elu_head(i)
             if i + 1 == LAST:
-                for earlier in range(LAST):
-                    elu_tail(earlier)
-        elu_tail(LAST)
+                elu_tail(0)
+        for i in range(1, PAIRS):
+            elu_tail(i)

@@ -17,6 +17,7 @@ EXPERTS = 8
 LATENT = 128
 FEATURES = 512
 PACK = 4
+WORDS = 2
 HIDDEN = 384
 EPS = 1e-5
 TILES = ROWS // P
@@ -26,6 +27,7 @@ HALF = TILES // 2
 N_WIDE = 256
 SPLIT = 2
 SIDE_EXPERTS = 2
+VECTOR_STAT_PAIRS = 3
 OWN_EXPERTS = EXPERTS - SIDE_EXPERTS
 
 FLOPS = 2 * ROWS * FEATURES * HIDDEN * EXPERTS + 2 * ROWS * EXPERTS * HIDDEN
@@ -49,6 +51,7 @@ def tile_gatingmixeddecoder_pa_e_kernel(tc, z, c, gate_logits, w0_words, w0_scal
         w_planes = keep.tile([P, EXPERTS, HIDDEN], U8, align_bytes=64)
         b_rep = keep.tile([P, HIDDEN], BF16)
         ident = keep.tile([P, P], BF16)
+        ident_f32 = keep.tile([P, P], F32)
         neg_half = keep.tile([P, PAIR], F32)
 
         nc.vector.memset(w_planes[:].bitcast(I32), 0)
@@ -66,6 +69,7 @@ def tile_gatingmixeddecoder_pa_e_kernel(tc, z, c, gate_logits, w0_words, w0_scal
         for e in range(0, EXPERTS, 2):
             nc.sync.dma_start(out=w_words[:, e : e + 2, :].bitcast(I32), in_=words_dram[:, e : e + 2, :])
         make_identity(nc, ident[:])
+        make_identity(nc, ident_f32[:])
         nc.gpsimd.dma_start(out=b_rep[:], in_=b0.unsqueeze(0).to_broadcast([P // EXPERTS, EXPERTS, HIDDEN]))
 
         def tiles_of(i):
@@ -85,6 +89,33 @@ def tile_gatingmixeddecoder_pa_e_kernel(tc, z, c, gate_logits, w0_words, w0_scal
         )
         expd = keep.tile([P, TILES, EXPERTS], F32)
         nc.scalar.activation(out=expd[:], in_=shifted[:], func=ACT.Exp)
+
+        mean_var = keep.tile([P, TILES, 2], F32)
+        sq_sum = keep.tile([P, TILES], F32)
+        var_eps = keep.tile([P, TILES], F32)
+        rstd = keep.tile([P, TILES], F32)
+        for i in range(VECTOR_STAT_PAIRS, PAIRS):
+            for t in tiles_of(i):
+                scrap = work.tile([P, FEATURES], BF16, tag="scrap")
+                nc.scalar.activation(
+                    out=scrap[:], in_=x_sb[:, t, :], func=ACT.Copy, scale=1.0 / FEATURES, accum_out=mean_var[:, t, 0:1]
+                )
+            for t in tiles_of(i):
+                scrap = work.tile([P, FEATURES], BF16, tag="scrap")
+                nc.scalar.activation(
+                    out=scrap[:], in_=x_sb[:, t, :], func=ACT.Square, scale=-1.0, bias=mean_var[:, t, 0:1],
+                    accum_out=sq_sum[:, t : t + 1],
+                )
+            nc.gpsimd.tensor_scalar(
+                out=var_eps[:, pair_of(i)],
+                in0=sq_sum[:, pair_of(i)],
+                scalar1=1.0 / FEATURES,
+                scalar2=EPS,
+                op0=ALU.mult,
+                op1=ALU.add,
+            )
+            nc.gpsimd.tensor_tensor(out=rstd[:, pair_of(i)], in0=var_eps[:, pair_of(i)], in1=neg_half[:], op=ALU.pow)
+
         exp_sum = keep.tile([P, TILES], F32)
         nc.vector.tensor_reduce(out=exp_sum[:], in_=expd[:], axis=AXIS.X, op=ALU.add)
         inv_sum = keep.tile([P, TILES], F32)
@@ -110,33 +141,37 @@ def tile_gatingmixeddecoder_pa_e_kernel(tc, z, c, gate_logits, w0_words, w0_scal
         for t in range(TILES):
             nc.scalar.activation(out=c_lhsT[:, t, :], in_=c_flip[:], func=ACT.Copy, scale=own_tile[:, t : t + 1])
         side = keep.tile([P, TILES, HIDDEN], F32)
-        for t in range(TILES):
-            bias_ps = lent.tile([P, HIDDEN], F32, tag="lent")
-            nc.tensor.matmul(out=bias_ps[:], lhsT=c_lhsT[:, t, :], rhs=b_rep[:], start=True, stop=True)
-            nc.scalar.copy(out=side[:, t, :], in_=bias_ps[:])
+
+        def bias(i):
+            for t in tiles_of(i):
+                bias_ps = lent.tile([P, HIDDEN], F32, tag="lent")
+                nc.tensor.matmul(out=bias_ps[:], lhsT=c_lhsT[:, t, :], rhs=b_rep[:], start=True, stop=True)
+                nc.scalar.copy(out=side[:, t, :], in_=bias_ps[:])
+
+        bias(0)
 
         stats = keep.tile([P, TILES, 6], F32)
-        mean_var = keep.tile([P, TILES, 2], F32)
-        var_eps = keep.tile([P, TILES], F32)
-        rstd = keep.tile([P, TILES], F32)
         inp = keep.tile([P, TILES, FEATURES], BF16)
         grouped = keep.tile([P, TILES, P, PACK], BF16, align_bytes=64)
         a_words = keep.tile([P, TILES, P], U32, align_bytes=64)
         a_planes = keep.tile([P, TILES, P], U8, align_bytes=64)
         for i in range(PAIRS):
-            for t in tiles_of(i):
-                nc.vector.bn_stats(out=stats[:, t, :], in_=x_sb[:, t, :])
-            for t in tiles_of(i):
-                nc.vector.bn_aggr(out=mean_var[:, t, :], in_=stats[:, t, :])
-            nc.gpsimd.tensor_scalar(
-                out=var_eps[:, pair_of(i)],
-                in0=mean_var[:, pair_of(i), 1],
-                scalar1=EPS,
-                scalar2=1.0,
-                op0=ALU.add,
-                op1=ALU.mult,
-            )
-            nc.gpsimd.tensor_tensor(out=rstd[:, pair_of(i)], in0=var_eps[:, pair_of(i)], in1=neg_half[:], op=ALU.pow)
+            if i < VECTOR_STAT_PAIRS:
+                for t in tiles_of(i):
+                    nc.vector.bn_stats(out=stats[:, t, :], in_=x_sb[:, t, :])
+                for t in tiles_of(i):
+                    nc.vector.bn_aggr(out=mean_var[:, t, :], in_=stats[:, t, :])
+                nc.gpsimd.tensor_scalar(
+                    out=var_eps[:, pair_of(i)],
+                    in0=mean_var[:, pair_of(i), 1],
+                    scalar1=EPS,
+                    scalar2=1.0,
+                    op0=ALU.add,
+                    op1=ALU.mult,
+                )
+                nc.gpsimd.tensor_tensor(
+                    out=rstd[:, pair_of(i)], in0=var_eps[:, pair_of(i)], in1=neg_half[:], op=ALU.pow
+                )
             for t in tiles_of(i):
                 nc.vector.tensor_scalar(
                     out=inp[:, t, :],
@@ -146,11 +181,18 @@ def tile_gatingmixeddecoder_pa_e_kernel(tc, z, c, gate_logits, w0_words, w0_scal
                     op0=ALU.subtract,
                     op1=ALU.mult,
                 )
-            flipped = flip.tile([P, PAIR, PACK, P], BF16, tag="flip")
+            flipped = flip.tile([P, PAIR, WORDS, P], F32, tag="flip")
             for a, t in enumerate(tiles_of(i)):
-                for j in range(PACK):
-                    nc.tensor.transpose(flipped[:, a, j, :], inp[:, t, j:FEATURES:PACK], ident[:])
-            nc.scalar.copy(out=grouped[:, pair_of(i)], in_=flipped[:].rearrange("p a j r -> p a r j"))
+                words = inp[:, t, :].bitcast(F32)
+                for u in range(WORDS):
+                    nc.tensor.transpose(flipped[:, a, u, :], words[:, u : FEATURES // 2 : WORDS], ident_f32[:])
+            nc.scalar.copy(
+                out=grouped[:, pair_of(i)]
+                .rearrange("p a r j -> p (a r j)")
+                .bitcast(F32)
+                .rearrange("p (a r u) -> p a r u", a=PAIR, u=WORDS),
+                in_=flipped[:].rearrange("p a u r -> p a r u"),
+            )
             nc.vector.quantize_mx(
                 out=a_words[:, pair_of(i), :].rearrange("p a r -> p (a r)").bitcast(FP8X4),
                 scales=a_planes[:, pair_of(i), :].rearrange("p a r -> p (a r)"),
@@ -210,13 +252,31 @@ def tile_gatingmixeddecoder_pa_e_kernel(tc, z, c, gate_logits, w0_words, w0_scal
                 )
                 nc.sync.dma_start(out=out_rows[:, t, :], in_=result[:, t, :])
 
+        one = keep.tile([P, 1], F32)
+        nc.vector.memset(one[:], 1.0)
+
+        def elu_beside(i):
+            for t in tiles_of(i):
+                raised = work.tile([P, HIDDEN], F32)
+                nc.scalar.activation(out=raised[:], in_=mixed[:, t, :], func=ACT.Exp)
+                short = work.tile([P, HIDDEN], F32)
+                nc.scalar.activation(out=short[:], in_=raised[:], func=ACT.Relu, scale=-1.0, bias=one[:])
+                above = work.tile([P, HIDDEN], F32)
+                nc.scalar.activation(out=above[:], in_=mixed[:, t, :], func=ACT.Relu)
+                nc.gpsimd.tensor_tensor(out=result[:, t, :], in0=above[:], in1=short[:], op=ALU.subtract)
+                nc.sync.dma_start(out=out_rows[:, t, :], in_=result[:, t, :])
+
         LAST = PAIRS - 1
+        BESIDE = 2
         for i in range(PAIRS):
             if i < LAST:
+                bias(i + 1)
                 side_terms(i + 1)
             own_terms(i, EXPERTS if i == 0 else OWN_EXPERTS)
-            elu_head(i)
+            if i >= BESIDE:
+                elu_head(i)
             if i + 1 == LAST:
-                elu_tail(0)
-        for i in range(1, PAIRS):
+                for earlier in range(BESIDE):
+                    elu_beside(earlier)
+        for i in range(BESIDE, PAIRS):
             elu_tail(i)

@@ -27,7 +27,7 @@ HALF = TILES // 2
 N_WIDE = 256
 SPLIT = 2
 SIDE_EXPERTS = 2
-VECTOR_STAT_PAIRS = 3
+VECTOR_STAT_PAIRS = 2
 OWN_EXPERTS = EXPERTS - SIDE_EXPERTS
 
 FLOPS = 2 * ROWS * FEATURES * HIDDEN * EXPERTS + 2 * ROWS * EXPERTS * HIDDEN
@@ -56,6 +56,8 @@ def tile_gatingmixeddecoder_pa_e_kernel(tc, z, c, gate_logits, w0_words, w0_scal
 
         nc.vector.memset(w_planes[:].bitcast(I32), 0)
         nc.vector.memset(neg_half[:], -0.5)
+        warm = keep.tile([P, 1], F32)
+        nc.scalar.activation(out=warm[:], in_=neg_half[:, 0:1], func=ACT.Exp)
 
         nc.sync.dma_start(out=gate_sb[:], in_=gate_rows)
         for h in range(TILES // HALF):
@@ -66,7 +68,7 @@ def tile_gatingmixeddecoder_pa_e_kernel(tc, z, c, gate_logits, w0_words, w0_scal
             nc.sync.dma_start(
                 out=w_planes[32 * quad : 32 * quad + 4].bitcast(I32), in_=scales_dram[4 * quad : 4 * quad + 4]
             )
-        for e in range(0, EXPERTS, 2):
+        for e in (OWN_EXPERTS, 0, 2, 4):
             nc.sync.dma_start(out=w_words[:, e : e + 2, :].bitcast(I32), in_=words_dram[:, e : e + 2, :])
         make_identity(nc, ident[:])
         make_identity(nc, ident_f32[:])

@@ -216,8 +216,11 @@ def tile_gatingmixeddecoder_pa_e_kernel(tc, z, c, gate_logits, w0_words, w0_scal
                     stop=True,
                 )
 
+        def own_experts(i):
+            return EXPERTS if i == 0 else OWN_EXPERTS - 1 if i == PAIRS - 1 else OWN_EXPERTS
+
         def side_terms(i):
-            for e in range(OWN_EXPERTS, EXPERTS):
+            for e in range(own_experts(i), EXPERTS):
                 for t in tiles_of(i):
                     y_lent = lent.tile([P, HIDDEN], F32, tag="lent")
                     product(y_lent, t, e)
@@ -274,7 +277,7 @@ def tile_gatingmixeddecoder_pa_e_kernel(tc, z, c, gate_logits, w0_words, w0_scal
             if i < LAST:
                 bias(i + 1)
                 side_terms(i + 1)
-            own_terms(i, EXPERTS if i == 0 else OWN_EXPERTS)
+            own_terms(i, own_experts(i))
             if i >= BESIDE:
                 elu_head(i)
             if i + 1 == LAST:

@@ -221,12 +221,17 @@ def tile_gatingmixeddecoder_pa_e_kernel(tc, z, c, gate_logits, w0_words, w0_scal
 
         def side_terms(i):
             for e in range(own_experts(i), EXPERTS):
-                for t in tiles_of(i):
+                part = work.tile([P, PAIR, HIDDEN], F32, tag="part")
+                for a, t in enumerate(tiles_of(i)):
                     y_lent = lent.tile([P, HIDDEN], F32, tag="lent")
                     product(y_lent, t, e)
-                    part = work.tile([P, HIDDEN], F32)
-                    nc.scalar.activation(out=part[:], in_=y_lent[:], func=ACT.Copy, scale=coeff[:, t, e : e + 1])
-                    nc.gpsimd.tensor_tensor(out=side[:, t, :], in0=side[:, t, :], in1=part[:], op=ALU.add)
+                    nc.scalar.activation(out=part[:, a, :], in_=y_lent[:], func=ACT.Copy, scale=coeff[:, t, e : e + 1])
+                    if i == 1:
+                        nc.gpsimd.tensor_tensor(out=side[:, t, :], in0=side[:, t, :], in1=part[:, a, :], op=ALU.add)
+                if i > 1:
+                    nc.gpsimd.tensor_tensor(
+                        out=side[:, pair_of(i), :], in0=side[:, pair_of(i), :], in1=part[:], op=ALU.add
+                    )
 
         def own_terms(i, experts):
             for e in range(experts):

@@ -234,7 +234,8 @@ def tile_gatingmixeddecoder_pa_e_kernel(tc, z, c, gate_logits, w0_words, w0_scal
                     )
 
         def own_terms(i, experts):
-            for e in range(experts):
+            order = [(e + OWN_EXPERTS) % EXPERTS for e in range(EXPERTS)] if i == 0 else list(range(experts))
+            for e in order:
                 for t in tiles_of(i):
                     y_own = own.tile([P, HIDDEN], F32, tag="own")
                     product(y_own, t, e)
@@ -242,7 +243,7 @@ def tile_gatingmixeddecoder_pa_e_kernel(tc, z, c, gate_logits, w0_words, w0_scal
                         out=mixed[:, t, :],
                         in0=y_own[:],
                         scalar=coeff[:, t, e : e + 1],
-                        in1=side[:, t, :] if e == 0 else mixed[:, t, :],
+                        in1=side[:, t, :] if e == order[0] else mixed[:, t, :],
                         op0=ALU.mult,
                         op1=ALU.add,
                     )

@@ -250,16 +250,17 @@ def tile_gatingmixeddecoder_pa_e_kernel(tc, z, c, gate_logits, w0_words, w0_scal
 
         grown = keep.tile([P, TILES, HIDDEN], F32)
 
+        kept = keep.tile([P, TILES, HIDDEN], F32)
+
         def elu_head(i):
             for t in tiles_of(i):
-                below = work.tile([P, HIDDEN], F32)
-                nc.scalar.activation(out=below[:], in_=mixed[:, t, :], func=ACT.Relu, scale=-1.0)
-                nc.scalar.activation(out=grown[:, t, :], in_=below[:], func=ACT.Exp, scale=-1.0)
+                nc.scalar.activation(out=grown[:, t, :], in_=mixed[:, t, :], func=ACT.Exp)
+                nc.vector.tensor_scalar_max(out=kept[:, t, :], in0=mixed[:, t, :], scalar1=0.0)
 
         def elu_tail(i):
             for t in tiles_of(i):
                 nc.vector.scalar_tensor_tensor(
-                    out=result[:, t, :], in0=grown[:, t, :], scalar=-1.0, in1=mixed[:, t, :], op0=ALU.add, op1=ALU.max
+                    out=result[:, t, :], in0=grown[:, t, :], scalar=-1.0, in1=kept[:, t, :], op0=ALU.add, op1=ALU.min
                 )
                 nc.sync.dma_start(out=out_rows[:, t, :], in_=result[:, t, :])
 
@@ -278,7 +279,7 @@ def tile_gatingmixeddecoder_pa_e_kernel(tc, z, c, gate_logits, w0_words, w0_scal
                 nc.sync.dma_start(out=out_rows[:, t, :], in_=result[:, t, :])
 
         LAST = PAIRS - 1
-        BESIDE = 2
+        BESIDE = 3
         for i in range(PAIRS):
             if i < LAST:
                 bias(i + 1)

@@ -27,7 +27,8 @@ HALF = TILES // 2
 N_WIDE = 256
 SPLIT = 2
 SIDE_EXPERTS = 2
-VECTOR_STAT_PAIRS = 2
+VECTOR_STAT_PAIRS = 3
+VECTOR_COPY_PAIRS = 2
 OWN_EXPERTS = EXPERTS - SIDE_EXPERTS
 
 FLOPS = 2 * ROWS * FEATURES * HIDDEN * EXPERTS + 2 * ROWS * EXPERTS * HIDDEN
@@ -64,6 +65,7 @@ def tile_gatingmixeddecoder_pa_e_kernel(tc, z, c, gate_logits, w0_words, w0_scal
             ts = slice(h * HALF, (h + 1) * HALF)
             nc.sync.dma_start(out=x_sb[:, ts, 0:LATENT], in_=z_rows[:, ts, :])
             nc.sync.dma_start(out=x_sb[:, ts, LATENT:FEATURES], in_=c_rows[:, ts, :])
+        nc.sync.dma_start(out=b_rep[:], in_=b0.unsqueeze(0).to_broadcast([P // EXPERTS, EXPERTS, HIDDEN]))
         for quad in range(4):
             nc.sync.dma_start(
                 out=w_planes[32 * quad : 32 * quad + 4].bitcast(I32), in_=scales_dram[4 * quad : 4 * quad + 4]
@@ -72,7 +74,6 @@ def tile_gatingmixeddecoder_pa_e_kernel(tc, z, c, gate_logits, w0_words, w0_scal
             nc.sync.dma_start(out=w_words[:, e : e + 2, :].bitcast(I32), in_=words_dram[:, e : e + 2, :])
         make_identity(nc, ident[:])
         make_identity(nc, ident_f32[:])
-        nc.gpsimd.dma_start(out=b_rep[:], in_=b0.unsqueeze(0).to_broadcast([P // EXPERTS, EXPERTS, HIDDEN]))
 
         def tiles_of(i):
             return range(i * PAIR, (i + 1) * PAIR)
@@ -81,99 +82,124 @@ def tile_gatingmixeddecoder_pa_e_kernel(tc, z, c, gate_logits, w0_words, w0_scal
             return slice(i * PAIR, (i + 1) * PAIR)
 
         gate_max = keep.tile([P, TILES], F32)
-        nc.vector.tensor_reduce(out=gate_max[:], in_=gate_sb[:], axis=AXIS.X, op=ALU.max)
         shifted = keep.tile([P, TILES, EXPERTS], F32)
-        nc.vector.tensor_tensor(
-            out=shifted[:],
-            in0=gate_sb[:],
-            in1=gate_max[:].unsqueeze(2).to_broadcast([P, TILES, EXPERTS]),
-            op=ALU.subtract,
-        )
         expd = keep.tile([P, TILES, EXPERTS], F32)
-        nc.scalar.activation(out=expd[:], in_=shifted[:], func=ACT.Exp)
-
+        exp_sum = keep.tile([P, TILES], F32)
+        inv_sum = keep.tile([P, TILES], F32)
+        coeff = keep.tile([P, TILES, EXPERTS], F32)
+        c_split = keep.tile([P, TILES, SPLIT, EXPERTS], BF16)
+        own_tile = keep.tile([P, TILES], F32)
+        c_lhsT = keep.tile([P, TILES, P], BF16)
+        side = keep.tile([P, TILES, HIDDEN], F32)
+        stats = keep.tile([P, TILES, 6], F32)
         mean_var = keep.tile([P, TILES, 2], F32)
         sq_sum = keep.tile([P, TILES], F32)
         var_eps = keep.tile([P, TILES], F32)
         rstd = keep.tile([P, TILES], F32)
-        for i in range(VECTOR_STAT_PAIRS, PAIRS):
+        inp = keep.tile([P, TILES, FEATURES], BF16)
+        grouped = keep.tile([P, TILES, P, PACK], BF16, align_bytes=64)
+        a_words = keep.tile([P, TILES, P], U32, align_bytes=64)
+        a_planes = keep.tile([P, TILES, P], U8, align_bytes=64)
+        mixed = keep.tile([P, TILES, HIDDEN], F32)
+        result = keep.tile([P, TILES, HIDDEN], F32)
+        grown = keep.tile([P, TILES, HIDDEN], F32)
+        kept = keep.tile([P, TILES, HIDDEN], F32)
+        one = keep.tile([P, 1], F32)
+        nc.vector.memset(one[:], 1.0)
+        flipped_of = {}
+        part_of = {}
+
+        def softmax_head():
+            nc.vector.tensor_reduce(out=gate_max[:], in_=gate_sb[:], axis=AXIS.X, op=ALU.max)
+            nc.vector.tensor_tensor(
+                out=shifted[:],
+                in0=gate_sb[:],
+                in1=gate_max[:].unsqueeze(2).to_broadcast([P, TILES, EXPERTS]),
+                op=ALU.subtract,
+            )
+            nc.scalar.activation(out=expd[:], in_=shifted[:], func=ACT.Exp)
+
+        def softmax_rest():
+            nc.vector.tensor_reduce(out=exp_sum[:], in_=expd[:], axis=AXIS.X, op=ALU.add)
+            nc.vector.reciprocal(out=inv_sum[:], in_=exp_sum[:])
+            nc.vector.tensor_tensor(
+                out=coeff[:],
+                in0=expd[:],
+                in1=inv_sum[:].unsqueeze(2).to_broadcast([P, TILES, EXPERTS]),
+                op=ALU.mult,
+            )
+
+        def split_and_turn():
+            nc.vector.tensor_copy(out=c_split[:, :, 0, :], in_=coeff[:])
+            nc.vector.tensor_tensor(out=c_split[:, :, 1, :], in0=coeff[:], in1=c_split[:, :, 0, :], op=ALU.subtract)
+            c_flip = flip.tile([P, P], BF16, tag="flip")
+            nc.tensor.transpose(c_flip[:], c_split[:].rearrange("p t h e -> p (t h e)"), ident[:])
+            return c_flip
+
+        def tile_marks():
+            nc.vector.tensor_reduce(
+                out=own_tile[:], in_=ident[:].rearrange("q (t j) -> q t j", t=TILES), axis=AXIS.X, op=ALU.add
+            )
+
+        def masks(c_flip):
+            for t in range(TILES):
+                nc.scalar.activation(out=c_lhsT[:, t, :], in_=c_flip[:], func=ACT.Copy, scale=own_tile[:, t : t + 1])
+
+        late = {"count": 0}
+
+        def borrowed(i):
+            if i >= VECTOR_COPY_PAIRS:
+                late["count"] = late["count"] + 1
+            if i >= VECTOR_COPY_PAIRS and late["count"] % 2 == 0:
+                bank = flip.tile([P, HIDDEN], F32, tag="flip")
+            else:
+                bank = lent.tile([P, HIDDEN], F32, tag="lent")
+            return bank
+
+        def bias_of(t):
+            bias_ps = borrowed(t // PAIR)
+            nc.tensor.matmul(out=bias_ps[:], lhsT=c_lhsT[:, t, :], rhs=b_rep[:], start=True, stop=True)
+            nc.scalar.copy(out=side[:, t, :], in_=bias_ps[:])
+
+        def bias(i):
+            for t in tiles_of(i):
+                bias_of(t)
+
+        def stats_on_vector(i):
+            for t in tiles_of(i):
+                nc.vector.bn_stats(out=stats[:, t, :], in_=x_sb[:, t, :])
+            for t in tiles_of(i):
+                nc.vector.bn_aggr(out=mean_var[:, t, :], in_=stats[:, t, :])
+
+        def means_on_scalar(i):
             for t in tiles_of(i):
                 scrap = work.tile([P, FEATURES], BF16, tag="scrap")
                 nc.scalar.activation(
                     out=scrap[:], in_=x_sb[:, t, :], func=ACT.Copy, scale=1.0 / FEATURES, accum_out=mean_var[:, t, 0:1]
                 )
+
+        def squares_on_scalar(i):
             for t in tiles_of(i):
                 scrap = work.tile([P, FEATURES], BF16, tag="scrap")
                 nc.scalar.activation(
                     out=scrap[:], in_=x_sb[:, t, :], func=ACT.Square, scale=-1.0, bias=mean_var[:, t, 0:1],
                     accum_out=sq_sum[:, t : t + 1],
                 )
-            nc.gpsimd.tensor_scalar(
-                out=var_eps[:, pair_of(i)],
-                in0=sq_sum[:, pair_of(i)],
-                scalar1=1.0 / FEATURES,
-                scalar2=EPS,
-                op0=ALU.mult,
-                op1=ALU.add,
-            )
+
+        def rstd_of(i):
+            if i < VECTOR_STAT_PAIRS:
+                nc.gpsimd.tensor_scalar(
+                    out=var_eps[:, pair_of(i)], in0=mean_var[:, pair_of(i), 1],
+                    scalar1=EPS, scalar2=1.0, op0=ALU.add, op1=ALU.mult,
+                )
+            else:
+                nc.gpsimd.tensor_scalar(
+                    out=var_eps[:, pair_of(i)], in0=sq_sum[:, pair_of(i)],
+                    scalar1=1.0 / FEATURES, scalar2=EPS, op0=ALU.mult, op1=ALU.add,
+                )
             nc.gpsimd.tensor_tensor(out=rstd[:, pair_of(i)], in0=var_eps[:, pair_of(i)], in1=neg_half[:], op=ALU.pow)
 
-        exp_sum = keep.tile([P, TILES], F32)
-        nc.vector.tensor_reduce(out=exp_sum[:], in_=expd[:], axis=AXIS.X, op=ALU.add)
-        inv_sum = keep.tile([P, TILES], F32)
-        nc.vector.reciprocal(out=inv_sum[:], in_=exp_sum[:])
-        coeff = keep.tile([P, TILES, EXPERTS], F32)
-        nc.vector.tensor_tensor(
-            out=coeff[:],
-            in0=expd[:],
-            in1=inv_sum[:].unsqueeze(2).to_broadcast([P, TILES, EXPERTS]),
-            op=ALU.mult,
-        )
-
-        c_split = keep.tile([P, TILES, SPLIT, EXPERTS], BF16)
-        nc.vector.tensor_copy(out=c_split[:, :, 0, :], in_=coeff[:])
-        nc.vector.tensor_tensor(out=c_split[:, :, 1, :], in0=coeff[:], in1=c_split[:, :, 0, :], op=ALU.subtract)
-        own_tile = keep.tile([P, TILES], F32)
-        nc.vector.tensor_reduce(
-            out=own_tile[:], in_=ident[:].rearrange("q (t j) -> q t j", t=TILES), axis=AXIS.X, op=ALU.add
-        )
-        c_flip = flip.tile([P, P], BF16, tag="flip")
-        nc.tensor.transpose(c_flip[:], c_split[:].rearrange("p t h e -> p (t h e)"), ident[:])
-        c_lhsT = keep.tile([P, TILES, P], BF16)
-        for t in range(TILES):
-            nc.scalar.activation(out=c_lhsT[:, t, :], in_=c_flip[:], func=ACT.Copy, scale=own_tile[:, t : t + 1])
-        side = keep.tile([P, TILES, HIDDEN], F32)
-
-        def bias(i):
-            for t in tiles_of(i):
-                bias_ps = lent.tile([P, HIDDEN], F32, tag="lent")
-                nc.tensor.matmul(out=bias_ps[:], lhsT=c_lhsT[:, t, :], rhs=b_rep[:], start=True, stop=True)
-                nc.scalar.copy(out=side[:, t, :], in_=bias_ps[:])
-
-        bias(0)
-
-        stats = keep.tile([P, TILES, 6], F32)
-        inp = keep.tile([P, TILES, FEATURES], BF16)
-        grouped = keep.tile([P, TILES, P, PACK], BF16, align_bytes=64)
-        a_words = keep.tile([P, TILES, P], U32, align_bytes=64)
-        a_planes = keep.tile([P, TILES, P], U8, align_bytes=64)
-        for i in range(PAIRS):
-            if i < VECTOR_STAT_PAIRS:
-                for t in tiles_of(i):
-                    nc.vector.bn_stats(out=stats[:, t, :], in_=x_sb[:, t, :])
-                for t in tiles_of(i):
-                    nc.vector.bn_aggr(out=mean_var[:, t, :], in_=stats[:, t, :])
-                nc.gpsimd.tensor_scalar(
-                    out=var_eps[:, pair_of(i)],
-                    in0=mean_var[:, pair_of(i), 1],
-                    scalar1=EPS,
-                    scalar2=1.0,
-                    op0=ALU.add,
-                    op1=ALU.mult,
-                )
-                nc.gpsimd.tensor_tensor(
-                    out=rstd[:, pair_of(i)], in0=var_eps[:, pair_of(i)], in1=neg_half[:], op=ALU.pow
-                )
+        def normalise(i):
             for t in tiles_of(i):
                 nc.vector.tensor_scalar(
                     out=inp[:, t, :],
@@ -183,26 +209,31 @@ def tile_gatingmixeddecoder_pa_e_kernel(tc, z, c, gate_logits, w0_words, w0_scal
                     op0=ALU.subtract,
                     op1=ALU.mult,
                 )
+
+        def turn(i):
             flipped = flip.tile([P, PAIR, WORDS, P], F32, tag="flip")
             for a, t in enumerate(tiles_of(i)):
                 words = inp[:, t, :].bitcast(F32)
                 for u in range(WORDS):
                     nc.tensor.transpose(flipped[:, a, u, :], words[:, u : FEATURES // 2 : WORDS], ident_f32[:])
-            nc.scalar.copy(
+            flipped_of[i] = flipped
+
+        def copy_out(i):
+            copier = nc.vector.tensor_copy if i < VECTOR_COPY_PAIRS else nc.scalar.copy
+            copier(
                 out=grouped[:, pair_of(i)]
                 .rearrange("p a r j -> p (a r j)")
                 .bitcast(F32)
                 .rearrange("p (a r u) -> p a r u", a=PAIR, u=WORDS),
-                in_=flipped[:].rearrange("p a u r -> p a r u"),
+                in_=flipped_of[i][:].rearrange("p a u r -> p a r u"),
             )
+
+        def quantise(i):
             nc.vector.quantize_mx(
                 out=a_words[:, pair_of(i), :].rearrange("p a r -> p (a r)").bitcast(FP8X4),
                 scales=a_planes[:, pair_of(i), :].rearrange("p a r -> p (a r)"),
                 in_=grouped[:, pair_of(i)].rearrange("p a r j -> p (a r j)"),
             )
-
-        mixed = keep.tile([P, TILES, HIDDEN], F32)
-        result = keep.tile([P, TILES, HIDDEN], F32)
 
         def product(y, t, e):
             for cols in (slice(0, N_WIDE), slice(N_WIDE, HIDDEN)):
@@ -219,38 +250,38 @@ def tile_gatingmixeddecoder_pa_e_kernel(tc, z, c, gate_logits, w0_words, w0_scal
         def own_experts(i):
             return EXPERTS if i == 0 else OWN_EXPERTS - 1 if i == PAIRS - 1 else OWN_EXPERTS
 
-        def side_terms(i):
-            for e in range(own_experts(i), EXPERTS):
+        def own_order(i):
+            return [(e + OWN_EXPERTS) % EXPERTS for e in range(EXPERTS)] if i == 0 else list(range(own_experts(i)))
+
+        def side_term(i, e, a, t):
+            if a == 0:
                 part = work.tile([P, PAIR, HIDDEN], F32, tag="part")
-                for a, t in enumerate(tiles_of(i)):
-                    y_lent = lent.tile([P, HIDDEN], F32, tag="lent")
-                    product(y_lent, t, e)
-                    nc.scalar.activation(out=part[:, a, :], in_=y_lent[:], func=ACT.Copy, scale=coeff[:, t, e : e + 1])
-                    if i == 1:
-                        nc.gpsimd.tensor_tensor(out=side[:, t, :], in0=side[:, t, :], in1=part[:, a, :], op=ALU.add)
-                if i > 1:
-                    nc.gpsimd.tensor_tensor(
-                        out=side[:, pair_of(i), :], in0=side[:, pair_of(i), :], in1=part[:], op=ALU.add
-                    )
+                part_of[(i, e)] = part
+            y_lent = borrowed(i)
+            product(y_lent, t, e)
+            nc.scalar.activation(
+                out=part_of[(i, e)][:, a, :], in_=y_lent[:], func=ACT.Copy, scale=coeff[:, t, e : e + 1]
+            )
 
-        def own_terms(i, experts):
-            order = [(e + OWN_EXPERTS) % EXPERTS for e in range(EXPERTS)] if i == 0 else list(range(experts))
-            for e in order:
-                for t in tiles_of(i):
-                    y_own = own.tile([P, HIDDEN], F32, tag="own")
-                    product(y_own, t, e)
-                    nc.vector.scalar_tensor_tensor(
-                        out=mixed[:, t, :],
-                        in0=y_own[:],
-                        scalar=coeff[:, t, e : e + 1],
-                        in1=side[:, t, :] if e == order[0] else mixed[:, t, :],
-                        op0=ALU.mult,
-                        op1=ALU.add,
-                    )
+        def add_tile(i, e, a, t):
+            nc.gpsimd.tensor_tensor(out=side[:, t, :], in0=side[:, t, :], in1=part_of[(i, e)][:, a, :], op=ALU.add)
 
-        grown = keep.tile([P, TILES, HIDDEN], F32)
+        def add_pair(i, e):
+            nc.gpsimd.tensor_tensor(
+                out=side[:, pair_of(i), :], in0=side[:, pair_of(i), :], in1=part_of[(i, e)][:], op=ALU.add
+            )
 
-        kept = keep.tile([P, TILES, HIDDEN], F32)
+        def own_term(i, e, t):
+            y_own = own.tile([P, HIDDEN], F32, tag="own")
+            product(y_own, t, e)
+            nc.vector.scalar_tensor_tensor(
+                out=mixed[:, t, :],
+                in0=y_own[:],
+                scalar=coeff[:, t, e : e + 1],
+                in1=side[:, t, :] if e == own_order(i)[0] else mixed[:, t, :],
+                op0=ALU.mult,
+                op1=ALU.add,
+            )
 
         def elu_head(i):
             for t in tiles_of(i):
@@ -264,31 +295,82 @@ def tile_gatingmixeddecoder_pa_e_kernel(tc, z, c, gate_logits, w0_words, w0_scal
                 )
                 nc.sync.dma_start(out=out_rows[:, t, :], in_=result[:, t, :])
 
-        one = keep.tile([P, 1], F32)
-        nc.vector.memset(one[:], 1.0)
-
-        def elu_beside(i):
-            for t in tiles_of(i):
-                raised = work.tile([P, HIDDEN], F32)
-                nc.scalar.activation(out=raised[:], in_=mixed[:, t, :], func=ACT.Exp)
-                short = work.tile([P, HIDDEN], F32)
-                nc.scalar.activation(out=short[:], in_=raised[:], func=ACT.Relu, scale=-1.0, bias=one[:])
-                above = work.tile([P, HIDDEN], F32)
-                nc.scalar.activation(out=above[:], in_=mixed[:, t, :], func=ACT.Relu)
-                nc.gpsimd.tensor_tensor(out=result[:, t, :], in0=above[:], in1=short[:], op=ALU.subtract)
-                nc.sync.dma_start(out=out_rows[:, t, :], in_=result[:, t, :])
+        def elu_beside(ts):
+            width = ts.stop - ts.start
+            raised = work.tile([P, PAIR, HIDDEN], F32)
+            nc.scalar.activation(out=raised[:, 0:width, :], in_=mixed[:, ts, :], func=ACT.Exp)
+            short = work.tile([P, PAIR, HIDDEN], F32)
+            nc.scalar.activation(out=short[:, 0:width, :], in_=raised[:, 0:width, :], func=ACT.Relu, scale=-1.0, bias=one[:])
+            above = work.tile([P, PAIR, HIDDEN], F32)
+            nc.scalar.activation(out=above[:, 0:width, :], in_=mixed[:, ts, :], func=ACT.Relu)
+            nc.gpsimd.tensor_tensor(
+                out=result[:, ts, :], in0=above[:, 0:width, :], in1=short[:, 0:width, :], op=ALU.subtract
+            )
+            nc.sync.dma_start(out=out_rows[:, ts, :], in_=result[:, ts, :])
 
         LAST = PAIRS - 1
         BESIDE = 3
-        for i in range(PAIRS):
-            if i < LAST:
-                bias(i + 1)
-                side_terms(i + 1)
-            own_terms(i, own_experts(i))
-            if i >= BESIDE:
-                elu_head(i)
-            if i + 1 == LAST:
-                for earlier in range(BESIDE):
-                    elu_beside(earlier)
-        for i in range(BESIDE, PAIRS):
-            elu_tail(i)
+
+        def side_steps(i):
+            steps = [[(bias_of, t)] for t in tiles_of(i)]
+            for e in range(own_experts(i), EXPERTS):
+                for a, t in enumerate(tiles_of(i)):
+                    if i == 1:
+                        steps = steps + [[(side_term, i, e, a, t), (add_tile, i, e, a, t)]]
+                    elif a + 1 < PAIR:
+                        steps = steps + [[(side_term, i, e, a, t)]]
+                    else:
+                        steps = steps + [[(side_term, i, e, a, t), (add_pair, i, e)]]
+            return steps
+
+        with tc.manual_schedule():
+            tile_marks()
+            softmax_head()
+            softmax_rest()
+            stats_on_vector(0)
+            rstd_of(0)
+            c_flip = split_and_turn()
+            stats_on_vector(1)
+            rstd_of(1)
+            means_on_scalar(LAST)
+            squares_on_scalar(LAST)
+            normalise(0)
+            turn(0)
+            stats_on_vector(2)
+            masks(c_flip)
+            bias(0)
+            rstd_of(LAST)
+            normalise(1)
+            copy_out(0)
+            turn(1)
+            quantise(0)
+            rstd_of(2)
+            copy_out(1)
+            first = side_steps(1)
+            waiting = [
+                [(quantise, 1)],
+                [(normalise, 3)],
+                first[0] + [(normalise, 2)],
+                first[1],
+                first[2],
+                first[3],
+                [(turn, 3), (copy_out, 3)],
+                [(turn, 2), (copy_out, 2)],
+                first[4] + [(quantise, 3)],
+                first[5] + [(quantise, 2)],
+            ] + side_steps(2) + side_steps(3)
+            dealt = 0
+            for i in range(PAIRS):
+                for e in own_order(i):
+                    for t in tiles_of(i):
+                        own_term(i, e, t)
+                        if dealt < len(waiting):
+                            for step in waiting[dealt]:
+                                step[0](*step[1:])
+                            dealt = dealt + 1
+                if i + 1 < BESIDE:
+                    waiting = waiting + [[(elu_beside, pair_of(i))]]
+                elif i < BESIDE:
+                    waiting = waiting + [[(elu_beside, slice(t, t + 1))] for t in tiles_of(i)]
+            elu_head(LAST)
+            elu_tail(LAST)

@@ -345,18 +345,19 @@ def tile_gatingmixeddecoder_pa_e_kernel(tc, z, c, gate_logits, w0_words, w0_scal
             turn(1)
             quantise(0)
             rstd_of(2)
+            normalise(LAST)
             copy_out(1)
             first = side_steps(1)
             waiting = [
                 [(quantise, 1)],
-                [(normalise, 3)],
-                first[0] + [(normalise, 2)],
-                first[1],
+                [(normalise, 2)],
+                first[0],
+                first[1] + [(turn, 3), (copy_out, 3)],
                 first[2],
                 first[3],
-                [(turn, 3), (copy_out, 3)],
+                [(quantise, 3)],
                 [(turn, 2), (copy_out, 2)],
-                first[4] + [(quantise, 3)],
+                first[4],
                 first[5] + [(quantise, 2)],
             ] + side_steps(2) + side_steps(3)
             dealt = 0

@@ -130,8 +130,8 @@ def tile_gatingmixeddecoder_pa_e_kernel(tc, z, c, gate_logits, w0_words, w0_scal
             )
 
         def split_and_turn():
-            nc.vector.tensor_copy(out=c_split[:, :, 0, :], in_=coeff[:])
-            nc.vector.tensor_tensor(out=c_split[:, :, 1, :], in0=coeff[:], in1=c_split[:, :, 0, :], op=ALU.subtract)
+            nc.gpsimd.tensor_copy(out=c_split[:, :, 0, :], in_=coeff[:])
+            nc.gpsimd.tensor_tensor(out=c_split[:, :, 1, :], in0=coeff[:], in1=c_split[:, :, 0, :], op=ALU.subtract)
             c_flip = flip.tile([P, P], BF16, tag="flip")
             nc.tensor.transpose(c_flip[:], c_split[:].rearrange("p t h e -> p (t h e)"), ident[:])
             return c_flip
@@ -327,9 +327,9 @@ def tile_gatingmixeddecoder_pa_e_kernel(tc, z, c, gate_logits, w0_words, w0_scal
             tile_marks()
             softmax_head()
             softmax_rest()
+            c_flip = split_and_turn()
             stats_on_vector(0)
             rstd_of(0)
-            c_flip = split_and_turn()
             stats_on_vector(1)
             rstd_of(1)
             means_on_scalar(LAST)

import concourse.mybir as mybir
from concourse.masks import make_identity

F32 = mybir.dt.float32
BF16 = mybir.dt.bfloat16
I32 = mybir.dt.int32
U32 = mybir.dt.uint32
U8 = mybir.dt.uint8
FP8X4 = mybir.dt.float8_e4m3fn_x4
ALU = mybir.AluOpType
ACT = mybir.ActivationFunctionType
AXIS = mybir.AxisListType

P = 128
ROWS = 1024
EXPERTS = 8
LATENT = 128
FEATURES = 512
PACK = 4
WORDS = 2
HIDDEN = 384
EPS = 1e-5
TILES = ROWS // P
PAIR = 2
PAIRS = TILES // PAIR
HALF = TILES // 2
N_WIDE = 256
SPLIT = 2
SIDE_EXPERTS = 2
VECTOR_STAT_PAIRS = 3
VECTOR_COPY_PAIRS = 2
OWN_EXPERTS = EXPERTS - SIDE_EXPERTS

FLOPS = 2 * ROWS * FEATURES * HIDDEN * EXPERTS + 2 * ROWS * EXPERTS * HIDDEN


def tile_gatingmixeddecoder_pa_e_kernel(tc, z, c, gate_logits, w0_words, w0_scales, b0, out):
    nc = tc.nc
    z_rows = z.rearrange("(p t) k -> p t k", t=TILES)
    c_rows = c.rearrange("(p t) k -> p t k", t=TILES)
    gate_rows = gate_logits.rearrange("(p t) e -> p t e", t=TILES)
    out_rows = out.rearrange("(p t) n -> p t n", t=TILES)
    words_dram = w0_words.rearrange("g p n t -> g p (n t)").bitcast(I32).rearrange("g p n -> p g n")
    scales_dram = w0_scales.bitcast(I32).rearrange("g q n -> q g n")

    with tc.tile_pool(name="keep", bufs=1) as keep, tc.tile_pool(name="work", bufs=4) as work, tc.psum_pool(
        name="flip", bufs=2
    ) as flip, tc.psum_pool(name="lent", bufs=2) as lent, tc.psum_pool(name="own", bufs=4) as own:
        x_sb = keep.tile([P, TILES, FEATURES], BF16)
        gate_sb = keep.tile([P, TILES, EXPERTS], BF16)
        w_words = keep.tile([P, EXPERTS, HIDDEN], U32, align_bytes=64)
        w_planes = keep.tile([P, EXPERTS, HIDDEN], U8, align_bytes=64)
        b_rep = keep.tile([P, HIDDEN], BF16)
        ident = keep.tile([P, P], BF16)
        ident_f32 = keep.tile([P, P], F32)
        neg_half = keep.tile([P, PAIR], F32)

        nc.vector.memset(w_planes[:].bitcast(I32), 0)
        nc.vector.memset(neg_half[:], -0.5)
        warm = keep.tile([P, 1], F32)
        nc.scalar.activation(out=warm[:], in_=neg_half[:, 0:1], func=ACT.Exp)

        nc.sync.dma_start(out=gate_sb[:], in_=gate_rows)
        for h in range(TILES // HALF):
            ts = slice(h * HALF, (h + 1) * HALF)
            nc.sync.dma_start(out=x_sb[:, ts, 0:LATENT], in_=z_rows[:, ts, :])
            nc.sync.dma_start(out=x_sb[:, ts, LATENT:FEATURES], in_=c_rows[:, ts, :])
        nc.sync.dma_start(out=b_rep[:], in_=b0.unsqueeze(0).to_broadcast([P // EXPERTS, EXPERTS, HIDDEN]))
        for quad in range(4):
            nc.sync.dma_start(
                out=w_planes[32 * quad : 32 * quad + 4].bitcast(I32), in_=scales_dram[4 * quad : 4 * quad + 4]
            )
        for e in (OWN_EXPERTS, 0, 2, 4):
            nc.sync.dma_start(out=w_words[:, e : e + 2, :].bitcast(I32), in_=words_dram[:, e : e + 2, :])
        make_identity(nc, ident[:])
        make_identity(nc, ident_f32[:])

        def tiles_of(i):
            return range(i * PAIR, (i + 1) * PAIR)

        def pair_of(i):
            return slice(i * PAIR, (i + 1) * PAIR)

        gate_max = keep.tile([P, TILES], F32)
        shifted = keep.tile([P, TILES, EXPERTS], F32)
        expd = keep.tile([P, TILES, EXPERTS], F32)
        exp_sum = keep.tile([P, TILES], F32)
        inv_sum = keep.tile([P, TILES], F32)
        coeff = keep.tile([P, TILES, EXPERTS], F32)
        c_split = keep.tile([P, TILES, SPLIT, EXPERTS], BF16)
        own_tile = keep.tile([P, TILES], F32)
        c_lhsT = keep.tile([P, TILES, P], BF16)
        side = keep.tile([P, TILES, HIDDEN], F32)
        stats = keep.tile([P, TILES, 6], F32)
        mean_var = keep.tile([P, TILES, 2], F32)
        sq_sum = keep.tile([P, TILES], F32)
        var_eps = keep.tile([P, TILES], F32)
        rstd = keep.tile([P, TILES], F32)
        inp = keep.tile([P, TILES, FEATURES], BF16)
        grouped = keep.tile([P, TILES, P, PACK], BF16, align_bytes=64)
        a_words = keep.tile([P, TILES, P], U32, align_bytes=64)
        a_planes = keep.tile([P, TILES, P], U8, align_bytes=64)
        mixed = keep.tile([P, TILES, HIDDEN], F32)
        result = keep.tile([P, TILES, HIDDEN], F32)
        grown = keep.tile([P, TILES, HIDDEN], F32)
        kept = keep.tile([P, TILES, HIDDEN], F32)
        one = keep.tile([P, 1], F32)
        nc.vector.memset(one[:], 1.0)
        flipped_of = {}
        part_of = {}

        def softmax_head():
            nc.vector.tensor_reduce(out=gate_max[:], in_=gate_sb[:], axis=AXIS.X, op=ALU.max)
            nc.vector.tensor_tensor(
                out=shifted[:],
                in0=gate_sb[:],
                in1=gate_max[:].unsqueeze(2).to_broadcast([P, TILES, EXPERTS]),
                op=ALU.subtract,
            )
            nc.scalar.activation(out=expd[:], in_=shifted[:], func=ACT.Exp)

        def softmax_rest():
            nc.vector.tensor_reduce(out=exp_sum[:], in_=expd[:], axis=AXIS.X, op=ALU.add)
            nc.vector.reciprocal(out=inv_sum[:], in_=exp_sum[:])
            nc.vector.tensor_tensor(
                out=coeff[:],
                in0=expd[:],
                in1=inv_sum[:].unsqueeze(2).to_broadcast([P, TILES, EXPERTS]),
                op=ALU.mult,
            )

        def split_and_turn():
            nc.gpsimd.tensor_copy(out=c_split[:, :, 0, :], in_=coeff[:])
            nc.gpsimd.tensor_tensor(out=c_split[:, :, 1, :], in0=coeff[:], in1=c_split[:, :, 0, :], op=ALU.subtract)
            c_flip = flip.tile([P, P], BF16, tag="flip")
            nc.tensor.transpose(c_flip[:], c_split[:].rearrange("p t h e -> p (t h e)"), ident[:])
            return c_flip

        def tile_marks():
            nc.vector.tensor_reduce(
                out=own_tile[:], in_=ident[:].rearrange("q (t j) -> q t j", t=TILES), axis=AXIS.X, op=ALU.add
            )

        def masks(c_flip):
            for t in range(TILES):
                nc.scalar.activation(out=c_lhsT[:, t, :], in_=c_flip[:], func=ACT.Copy, scale=own_tile[:, t : t + 1])

        late = {"count": 0}

        def borrowed(i):
            if i >= VECTOR_COPY_PAIRS:
                late["count"] = late["count"] + 1
            if i >= VECTOR_COPY_PAIRS and late["count"] % 2 == 0:
                bank = flip.tile([P, HIDDEN], F32, tag="flip")
            else:
                bank = lent.tile([P, HIDDEN], F32, tag="lent")
            return bank

        def bias_of(t):
            bias_ps = borrowed(t // PAIR)
            nc.tensor.matmul(out=bias_ps[:], lhsT=c_lhsT[:, t, :], rhs=b_rep[:], start=True, stop=True)
            nc.scalar.copy(out=side[:, t, :], in_=bias_ps[:])

        def bias(i):
            for t in tiles_of(i):
                bias_of(t)

        def stats_on_vector(i):
            for t in tiles_of(i):
                nc.vector.bn_stats(out=stats[:, t, :], in_=x_sb[:, t, :])
            for t in tiles_of(i):
                nc.vector.bn_aggr(out=mean_var[:, t, :], in_=stats[:, t, :])

        def means_on_scalar(i):
            for t in tiles_of(i):
                scrap = work.tile([P, FEATURES], BF16, tag="scrap")
                nc.scalar.activation(
                    out=scrap[:], in_=x_sb[:, t, :], func=ACT.Copy, scale=1.0 / FEATURES, accum_out=mean_var[:, t, 0:1]
                )

        def squares_on_scalar(i):
            for t in tiles_of(i):
                scrap = work.tile([P, FEATURES], BF16, tag="scrap")
                nc.scalar.activation(
                    out=scrap[:], in_=x_sb[:, t, :], func=ACT.Square, scale=-1.0, bias=mean_var[:, t, 0:1],
                    accum_out=sq_sum[:, t : t + 1],
                )

        def rstd_of(i):
            if i < VECTOR_STAT_PAIRS:
                nc.gpsimd.tensor_scalar(
                    out=var_eps[:, pair_of(i)], in0=mean_var[:, pair_of(i), 1],
                    scalar1=EPS, scalar2=1.0, op0=ALU.add, op1=ALU.mult,
                )
            else:
                nc.gpsimd.tensor_scalar(
                    out=var_eps[:, pair_of(i)], in0=sq_sum[:, pair_of(i)],
                    scalar1=1.0 / FEATURES, scalar2=EPS, op0=ALU.mult, op1=ALU.add,
                )
            nc.gpsimd.tensor_tensor(out=rstd[:, pair_of(i)], in0=var_eps[:, pair_of(i)], in1=neg_half[:], op=ALU.pow)

        def normalise(i):
            for t in tiles_of(i):
                nc.vector.tensor_scalar(
                    out=inp[:, t, :],
                    in0=x_sb[:, t, :],
                    scalar1=mean_var[:, t, 0:1],
                    scalar2=rstd[:, t : t + 1],
                    op0=ALU.subtract,
                    op1=ALU.mult,
                )

        def turn(i):
            flipped = flip.tile([P, PAIR, WORDS, P], F32, tag="flip")
            for a, t in enumerate(tiles_of(i)):
                words = inp[:, t, :].bitcast(F32)
                for u in range(WORDS):
                    nc.tensor.transpose(flipped[:, a, u, :], words[:, u : FEATURES // 2 : WORDS], ident_f32[:])
            flipped_of[i] = flipped

        def copy_out(i):
            copier = nc.vector.tensor_copy if i < VECTOR_COPY_PAIRS else nc.scalar.copy
            copier(
                out=grouped[:, pair_of(i)]
                .rearrange("p a r j -> p (a r j)")
                .bitcast(F32)
                .rearrange("p (a r u) -> p a r u", a=PAIR, u=WORDS),
                in_=flipped_of[i][:].rearrange("p a u r -> p a r u"),
            )

        def quantise(i):
            nc.vector.quantize_mx(
                out=a_words[:, pair_of(i), :].rearrange("p a r -> p (a r)").bitcast(FP8X4),
                scales=a_planes[:, pair_of(i), :].rearrange("p a r -> p (a r)"),
                in_=grouped[:, pair_of(i)].rearrange("p a r j -> p (a r j)"),
            )

        def product(y, t, e):
            for cols in (slice(0, N_WIDE), slice(N_WIDE, HIDDEN)):
                nc.tensor.matmul_mx(
                    out=y[:, cols],
                    lhsT=a_words[:, t, :].bitcast(FP8X4),
                    lhsT_scale=a_planes[:, t, :],
                    rhs=w_words[:, e, cols].bitcast(FP8X4),
                    rhs_scale=w_planes[:, e, cols],
                    start=True,
                    stop=True,
                )

        def own_experts(i):
            return EXPERTS if i == 0 else OWN_EXPERTS - 1 if i == PAIRS - 1 else OWN_EXPERTS

        def own_order(i):
            return [(e + OWN_EXPERTS) % EXPERTS for e in range(EXPERTS)] if i == 0 else list(range(own_experts(i)))

        def side_term(i, e, a, t):
            if a == 0:
                part = work.tile([P, PAIR, HIDDEN], F32, tag="part")
                part_of[(i, e)] = part
            y_lent = borrowed(i)
            product(y_lent, t, e)
            nc.scalar.activation(
                out=part_of[(i, e)][:, a, :], in_=y_lent[:], func=ACT.Copy, scale=coeff[:, t, e : e + 1]
            )

        def add_tile(i, e, a, t):
            nc.gpsimd.tensor_tensor(out=side[:, t, :], in0=side[:, t, :], in1=part_of[(i, e)][:, a, :], op=ALU.add)

        def add_pair(i, e):
            nc.gpsimd.tensor_tensor(
                out=side[:, pair_of(i), :], in0=side[:, pair_of(i), :], in1=part_of[(i, e)][:], op=ALU.add
            )

        def own_term(i, e, t):
            y_own = own.tile([P, HIDDEN], F32, tag="own")
            product(y_own, t, e)
            nc.vector.scalar_tensor_tensor(
                out=mixed[:, t, :],
                in0=y_own[:],
                scalar=coeff[:, t, e : e + 1],
                in1=side[:, t, :] if e == own_order(i)[0] else mixed[:, t, :],
                op0=ALU.mult,
                op1=ALU.add,
            )

        def elu_head(i):
            for t in tiles_of(i):
                nc.scalar.activation(out=grown[:, t, :], in_=mixed[:, t, :], func=ACT.Exp)
                nc.vector.tensor_scalar_max(out=kept[:, t, :], in0=mixed[:, t, :], scalar1=0.0)

        def elu_tail(i):
            for t in tiles_of(i):
                nc.vector.scalar_tensor_tensor(
                    out=result[:, t, :], in0=grown[:, t, :], scalar=-1.0, in1=kept[:, t, :], op0=ALU.add, op1=ALU.min
                )
                nc.sync.dma_start(out=out_rows[:, t, :], in_=result[:, t, :])

        def elu_beside(ts):
            width = ts.stop - ts.start
            raised = work.tile([P, PAIR, HIDDEN], F32)
            nc.scalar.activation(out=raised[:, 0:width, :], in_=mixed[:, ts, :], func=ACT.Exp)
            short = work.tile([P, PAIR, HIDDEN], F32)
            nc.scalar.activation(out=short[:, 0:width, :], in_=raised[:, 0:width, :], func=ACT.Relu, scale=-1.0, bias=one[:])
            above = work.tile([P, PAIR, HIDDEN], F32)
            nc.scalar.activation(out=above[:, 0:width, :], in_=mixed[:, ts, :], func=ACT.Relu)
            nc.gpsimd.tensor_tensor(
                out=result[:, ts, :], in0=above[:, 0:width, :], in1=short[:, 0:width, :], op=ALU.subtract
            )
            nc.sync.dma_start(out=out_rows[:, ts, :], in_=result[:, ts, :])

        LAST = PAIRS - 1
        BESIDE = 3

        def side_steps(i):
            steps = [[(bias_of, t)] for t in tiles_of(i)]
            for e in range(own_experts(i), EXPERTS):
                for a, t in enumerate(tiles_of(i)):
                    if i == 1:
                        steps = steps + [[(side_term, i, e, a, t), (add_tile, i, e, a, t)]]
                    elif a + 1 < PAIR:
                        steps = steps + [[(side_term, i, e, a, t)]]
                    else:
                        steps = steps + [[(side_term, i, e, a, t), (add_pair, i, e)]]
            return steps

        with tc.manual_schedule():
            tile_marks()
            softmax_head()
            softmax_rest()
            c_flip = split_and_turn()
            stats_on_vector(0)
            rstd_of(0)
            stats_on_vector(1)
            rstd_of(1)
            means_on_scalar(LAST)
            squares_on_scalar(LAST)
            normalise(0)
            turn(0)
            stats_on_vector(2)
            masks(c_flip)
            bias(0)
            rstd_of(LAST)
            normalise(1)
            copy_out(0)
            turn(1)
            quantise(0)
            rstd_of(2)
            normalise(LAST)
            copy_out(1)
            first = side_steps(1)
            waiting = [
                [(quantise, 1)],
                [(normalise, 2)],
                first[0],
                first[1] + [(turn, 3), (copy_out, 3)],
                first[2],
                first[3],
                [(quantise, 3)],
                [(turn, 2), (copy_out, 2)],
                first[4],
                first[5] + [(quantise, 2)],
            ] + side_steps(2) + side_steps(3)
            dealt = 0
            for i in range(PAIRS):
                for e in own_order(i):
                    for t in tiles_of(i):
                        own_term(i, e, t)
                        if dealt < len(waiting):
                            for step in waiting[dealt]:
                                step[0](*step[1:])
                            dealt = dealt + 1
                if i + 1 < BESIDE:
                    waiting = waiting + [[(elu_beside, pair_of(i))]]
                elif i < BESIDE:
                    waiting = waiting + [[(elu_beside, slice(t, t + 1))] for t in tiles_of(i)]
            elu_head(LAST)
            elu_tail(LAST)
